import numpy as np
import ml_dtypes


def mxq(x, axis, fmt="e4m3"):
    dtype, down = {"e4m3": (ml_dtypes.float8_e4m3fn, 7), "e5m2": (ml_dtypes.float8_e5m2, 14)}[fmt]
    v = np.moveaxis(np.asarray(x, np.float32).astype(ml_dtypes.bfloat16).astype(np.float64), axis, -1)
    blocks = v.reshape(v.shape[:-1] + (-1, 32))
    amax = np.abs(blocks).max(-1, keepdims=True)
    byte = np.maximum(np.where(amax > 0, np.frexp(amax)[1] - 1 + 127, 0) - down, 1)
    scale = np.exp2(byte - 127.0)
    codes = (blocks / scale).astype(np.float32).astype(dtype).astype(np.float64)
    return np.moveaxis((codes * scale).reshape(v.shape), -1, axis)


WIDE = False


def mx_kscale(k):
    if not WIDE:
        return np.ones(k)
    levels = np.array([10, -10, 5, -5, 0])
    a = np.random.permutation(np.resize(levels, k // 512 * 4)).reshape(k // 512, 4)
    idx = np.arange(k)
    return np.exp2(a[idx // 512, idx % 128 // 32])


BF16 = ml_dtypes.bfloat16


def bf(x):
    return np.asarray(x, np.float32).astype(BF16)


def f64(x):
    return np.asarray(x).astype(np.float64)


E2M1 = np.array([0.0, 0.5, 1.0, 1.5, 2.0, 3.0, 4.0, 6.0, -0.0, -0.5, -1.0, -1.5, -2.0, -3.0, -4.0, -6.0])


def pack_weight(w, fmt):
    k, n = w.shape
    w = f64(bf(w)).reshape(k // 32, 32, n)
    amax = np.abs(w).max(1)
    if fmt == "e4m3":
        byte = np.frexp(amax)[1] - 1 + 127 - 7
    else:
        mant, ex = np.frexp(amax / 6.0)
        byte = np.where(mant > 0.5, ex, ex - 1) + 127
    byte = np.clip(np.where(amax > 0, byte, 1), 1, 254)
    scaled = (w * np.exp2(127.0 - byte)[:, None, :]).reshape(k, n).astype(np.float32)
    by_word = np.ascontiguousarray(scaled.reshape(k // 512, 128, 4, n).transpose(0, 1, 3, 2))
    if fmt == "e4m3":
        words = by_word.astype(ml_dtypes.float8_e4m3fn).view(np.uint8)
    else:
        c = by_word.astype(ml_dtypes.float4_e2m1fn).view(np.uint8) & 0xF
        words = c[..., 0::2] | (c[..., 1::2] << 4)
    return np.ascontiguousarray(words), np.ascontiguousarray(byte.astype(np.uint8).reshape(k // 512, 16, n))


def unpack_weight(words, scales, fmt):
    g, p, n, _ = words.shape
    if fmt == "e4m3":
        vals = np.ascontiguousarray(words).view(ml_dtypes.float8_e4m3fn).astype(np.float64)
    else:
        nib = np.empty((g, p, n, 4), np.uint8)
        nib[..., 0::2] = words & 0xF
        nib[..., 1::2] = words >> 4
        vals = E2M1[nib]
    vals = vals * np.repeat(np.exp2(scales.astype(np.float64) - 127.0), 8, axis=1)[..., None]
    return vals.transpose(0, 1, 3, 2).reshape(g * 512, n)

def pack4(w):
    words, scales = pack_weight(w, "e2m1")
    return words.reshape(words.shape[0], 128, -1), scales


def unpack4(words, scales):
    return unpack_weight(words.reshape(words.shape[0], 128, -1, 2), scales, "e2m1")


B, I, H = 4096, 512, 512
EPS = 1e-5


def ln(v):
    mu = v.mean(-1, keepdims=True)
    var = np.square(v - mu).mean(-1, keepdims=True)
    return (v - mu) / np.sqrt(var + EPS)


def sigmoid(v):
    return 1.0 / (1.0 + np.exp(-v))


def setup_inputs():
    s = mx_kscale(I)
    x = bf(np.random.standard_normal((B, I)) * s)
    h = bf(np.random.standard_normal((B, H)))
    r = bf(sigmoid(np.sqrt(2.0) * np.random.standard_normal((B, H))))
    z = bf(sigmoid(np.sqrt(2.0) * np.random.standard_normal((B, H))))
    W_in = np.random.standard_normal((H, I)) / np.sqrt(I) / s
    b_in = bf(np.random.standard_normal(H) * 0.5)
    W_hn = np.random.standard_normal((H, H)) / np.sqrt(H)
    b_hn = bf(np.random.standard_normal(H) * 0.5)
    W_in_words, W_in_scales = pack4(np.ascontiguousarray(W_in.T))
    W_hn_words, W_hn_scales = pack4(np.ascontiguousarray(W_hn.T))
    return {"x": x,
            "h": h,
            "r": r,
            "z": z,
            "W_in_words": W_in_words,
            "W_in_scales": W_in_scales,
            "b_in": b_in,
            "W_hn_words": W_hn_words,
            "W_hn_scales": W_hn_scales,
            "b_hn": b_hn}


def reference(x, h, r, z, W_in_words, W_in_scales, b_in, W_hn_words, W_hn_scales, b_hn):
    h = f64(h)
    r, z = f64(r), f64(z)
    i_n = ln((mxq(f64(x), 1, "e4m3") @ unpack4(W_in_words, W_in_scales)) + f64(b_in))
    h_n = ln((mxq(h, 1, "e4m3") @ unpack4(W_hn_words, W_hn_scales)) + f64(b_hn))
    n = np.tanh(i_n + r * h_n)
    return (1.0 - z) * n + z * h

@@ -1,0 +1,239 @@
+from contextlib import ExitStack
+
+import concourse.mybir as mybir
+from concourse.masks import make_identity
+
+F32 = mybir.dt.float32
+BF16 = mybir.dt.bfloat16
+I32 = mybir.dt.int32
+U32 = mybir.dt.uint32
+U8 = mybir.dt.uint8
+FP8X4 = mybir.dt.float8_e4m3fn_x4
+FP4X4 = mybir.dt.float4_e2m1fn_x4
+ALU = mybir.AluOpType
+ACT = mybir.ActivationFunctionType
+
+P = 128
+PACK = 4
+ROWS = 4096
+WIDTH = 512
+TILES = 4
+GROUPS = ROWS // (P * TILES)
+EPS = 1e-5
+FLOPS = 2 * 2 * ROWS * WIDTH * WIDTH
+
+
+def tile_layernormgrucell_pb_t_kernel(
+    tc, x, h, r, z, W_in_words, W_in_scales, b_in, W_hn_words, W_hn_scales, b_hn, out
+):
+    nc = tc.nc
+    by_group = "(g p t) n -> g p t n"
+    x_groups = x.rearrange(by_group, p=P, t=TILES)
+    h_groups = h.rearrange(by_group, p=P, t=TILES)
+    r_groups = r.rearrange(by_group, p=P, t=TILES)
+    z_groups = z.rearrange(by_group, p=P, t=TILES)
+    out_groups = out.rearrange(by_group, p=P, t=TILES)
+    group_shape = [P, TILES, WIDTH]
+
+    with ExitStack() as ctx:
+        ctx.enter_context(tc.manual_schedule())
+        consts = ctx.enter_context(tc.tile_pool(name="consts", bufs=1))
+        pairs = ctx.enter_context(tc.tile_pool(name="pairs", bufs=2))
+        h_pool = ctx.enter_context(tc.tile_pool(name="h_pool", bufs=4))
+        scratch = ctx.enter_context(tc.tile_pool(name="scratch", bufs=4))
+        psum_turn = ctx.enter_context(tc.psum_pool(name="psum_turn", bufs=3))
+        psum_mm = ctx.enter_context(tc.psum_pool(name="psum_mm", bufs=5))
+
+        kept = {}
+
+        def load_activations(g):
+            x_sb = pairs.tile(group_shape, BF16, name="x_sb")
+            h_sb = h_pool.tile(group_shape, BF16, name="h_sb")
+            nc.sync.dma_start(out=x_sb[:], in_=x_groups[g])
+            nc.sync.dma_start(out=h_sb[:], in_=h_groups[g])
+            kept["x", g] = x_sb
+            kept["h", g] = h_sb
+
+        def load_gates(g):
+            r_sb = pairs.tile(group_shape, BF16, name="r_sb")
+            z_sb = pairs.tile(group_shape, BF16, name="z_sb")
+            nc.sync.dma_start(out=r_sb[:], in_=r_groups[g])
+            nc.sync.dma_start(out=z_sb[:], in_=z_groups[g])
+            kept["r", g] = r_sb
+            kept["z", g] = z_sb
+
+        def turn(g):
+            grouped = pairs.tile([P, TILES, 2, P, PACK], BF16, name="grouped", align_bytes=64)
+            for t in range(TILES):
+                turned = psum_turn.tile([P, 2, 2, P], F32, name="turned")
+                for path, rows_sb in enumerate((kept["x", g], kept["h", g])):
+                    row_words = rows_sb[:, t, :].bitcast(F32)
+                    for u in range(2):
+                        nc.tensor.transpose(
+                            turned[:, path, u, :], row_words[:, u : WIDTH // 2 : 2], ident[:]
+                        )
+                nc.scalar.copy(
+                    out=grouped[:, t].bitcast(F32),
+                    in_=turned[:].rearrange("p path u row -> p path row u"),
+                )
+            kept["grouped", g] = grouped
+
+        def quantise(g):
+            codes = pairs.tile([P, TILES, 2, P], U32, name="codes", align_bytes=64)
+            code_scales = pairs.tile([P, TILES, 2, P], U8, name="code_scales", align_bytes=64)
+            nc.vector.quantize_mx(
+                out=codes[:].rearrange("p t path row -> p (t path row)").bitcast(FP8X4),
+                scales=code_scales[:].rearrange("p t path row -> p (t path row)"),
+                in_=kept["grouped", g][:].rearrange("p t path row j -> p (t path row j)"),
+            )
+            kept["codes", g] = codes
+            kept["code_scales", g] = code_scales
+
+        def products(g):
+            pre = (
+                pairs.tile(group_shape, F32, name="i_pre"),
+                pairs.tile(group_shape, F32, name="h_pre"),
+            )
+            row_sum = pairs.tile([P, 2, TILES], F32, name="row_sum")
+            dev_sq_sum = pairs.tile([P, 2, TILES], F32, name="dev_sq_sum")
+            for t in range(TILES):
+                for path in range(2):
+                    product = psum_mm.tile([P, WIDTH], F32, name="product")
+                    nc.tensor.matmul_mx(
+                        out=product[:],
+                        lhsT=kept["codes", g][:, t, path, :].bitcast(FP8X4),
+                        lhsT_scale=kept["code_scales", g][:, t, path, :],
+                        rhs=w_words[path][:].bitcast(FP4X4),
+                        rhs_scale=w_scales[path][:],
+                        start=True,
+                        stop=True,
+                    )
+                    nc.vector.scalar_tensor_tensor(
+                        out=pre[path][:, t, :],
+                        in0=product[:],
+                        scalar=0.0,
+                        in1=bias_rows[path][:],
+                        op0=ALU.add,
+                        op1=ALU.add,
+                        accum_out=row_sum[:, path, t : t + 1],
+                    )
+                    dev_sq = scratch.tile([P, WIDTH], F32, name="dev_sq")
+                    nc.scalar.activation(
+                        out=dev_sq[:],
+                        in_=pre[path][:, t, :],
+                        func=ACT.Square,
+                        bias=row_sum[:, path, t : t + 1],
+                        scale=-1.0 * WIDTH,
+                        accum_out=dev_sq_sum[:, path, t : t + 1],
+                    )
+            neg_mean = pairs.tile([P, 2, TILES], F32, name="neg_mean")
+            var_eps = pairs.tile([P, 2, TILES], F32, name="var_eps")
+            rstd = pairs.tile([P, 2, TILES], F32, name="rstd")
+            std_i = pairs.tile([P, TILES], F32, name="std_i")
+            ratio = pairs.tile([P, TILES], F32, name="ratio")
+            shift_i = pairs.tile([P, TILES], F32, name="shift_i")
+            nc.gpsimd.tensor_scalar(
+                out=neg_mean[:], in0=row_sum[:], scalar1=-1.0 / WIDTH, scalar2=0.0,
+                op0=ALU.mult, op1=ALU.add,
+            )
+            nc.gpsimd.tensor_scalar(
+                out=var_eps[:], in0=dev_sq_sum[:], scalar1=1.0 / WIDTH**3, scalar2=EPS,
+                op0=ALU.mult, op1=ALU.add,
+            )
+            nc.gpsimd.tensor_tensor(out=rstd[:], in0=var_eps[:], in1=minus_half[:], op=ALU.pow)
+            nc.gpsimd.tensor_mul(out=std_i[:], in0=var_eps[:, 0, :], in1=rstd[:, 0, :])
+            nc.gpsimd.tensor_mul(out=ratio[:], in0=std_i[:], in1=rstd[:, 1, :])
+            nc.gpsimd.tensor_mul(out=shift_i[:], in0=neg_mean[:, 0, :], in1=rstd[:, 0, :])
+            kept["i_pre", g], kept["h_pre", g] = pre
+            kept["neg_mean", g] = neg_mean
+            kept["rstd", g] = rstd
+            kept["ratio", g] = ratio
+            kept["shift_i", g] = shift_i
+
+        def candidate(g):
+            gated = pairs.tile(group_shape, F32, name="gated")
+            mixed = pairs.tile(group_shape, F32, name="mixed")
+            cand = pairs.tile(group_shape, F32, name="cand")
+            for t in range(TILES):
+                nc.vector.scalar_tensor_tensor(
+                    out=gated[:, t, :],
+                    in0=kept["h_pre", g][:, t, :],
+                    scalar=kept["neg_mean", g][:, 1, t : t + 1],
+                    in1=kept["r", g][:, t, :],
+                    op0=ALU.add,
+                    op1=ALU.mult,
+                )
+            for t in range(TILES):
+                nc.vector.scalar_tensor_tensor(
+                    out=mixed[:, t, :],
+                    in0=gated[:, t, :],
+                    scalar=kept["ratio", g][:, t : t + 1],
+                    in1=kept["i_pre", g][:, t, :],
+                    op0=ALU.mult,
+                    op1=ALU.add,
+                )
+                nc.scalar.activation(
+                    out=cand[:, t, :],
+                    in_=mixed[:, t, :],
+                    func=ACT.Tanh,
+                    bias=kept["shift_i", g][:, t : t + 1],
+                    scale=kept["rstd", g][:, 0, t : t + 1],
+                )
+            kept["cand", g] = cand
+
+        def blend(g):
+            held = pairs.tile(group_shape, F32, name="held")
+            dropped = pairs.tile(group_shape, F32, name="dropped")
+            new_state = pairs.tile(group_shape, F32, name="new_state")
+            nc.vector.tensor_mul(out=held[:], in0=kept["z", g][:], in1=kept["h", g][:])
+            nc.vector.scalar_tensor_tensor(
+                out=dropped[:], in0=kept["z", g][:], scalar=1.0, in1=kept["cand", g][:],
+                op0=ALU.subtract, op1=ALU.mult,
+            )
+            nc.vector.tensor_sub(out=new_state[:], in0=held[:], in1=dropped[:])
+            nc.sync.dma_start(out=out_groups[g], in_=new_state[:])
+
+        load_activations(0)
+
+        ident = consts.tile([P, P], F32, name="ident")
+        make_identity(nc, ident[:])
+        minus_half = consts.tile([P, 2, TILES], F32, name="minus_half")
+        nc.gpsimd.memset(minus_half[:], -0.5)
+
+        w_words = []
+        w_scales = []
+        bias_rows = []
+        for path, words, scales, bias in (
+            ("i", W_in_words, W_in_scales, b_in),
+            ("h", W_hn_words, W_hn_scales, b_hn),
+        ):
+            words_sb = consts.tile([P, 2 * WIDTH], U8, name="w_words_" + path, align_bytes=64)
+            nc.sync.dma_start(out=words_sb[:].bitcast(I32), in_=words[0].bitcast(I32))
+            scales_sb = consts.tile([P, WIDTH], U8, name="w_scales_" + path, align_bytes=64)
+            nc.vector.memset(scales_sb[:].bitcast(I32), 0)
+            for quadrant in range(4):
+                nc.sync.dma_start(
+                    out=scales_sb[32 * quadrant : 32 * quadrant + 4, :].bitcast(I32),
+                    in_=scales[0, 4 * quadrant : 4 * quadrant + 4, :].bitcast(I32),
+                )
+            bias_sb = consts.tile([P, WIDTH], BF16, name="bias_" + path)
+            nc.sync.dma_start(out=bias_sb[:], in_=bias.partition_broadcast(P))
+            w_words.append(words_sb)
+            w_scales.append(scales_sb)
+            bias_rows.append(bias_sb)
+
+        for step in range(GROUPS + 2):
+            if step + 1 < GROUPS:
+                load_activations(step + 1)
+            if 1 <= step <= GROUPS:
+                load_gates(step - 1)
+            if step < GROUPS:
+                turn(step)
+            if step >= 2:
+                candidate(step - 2)
+            if 1 <= step <= GROUPS:
+                products(step - 1)
+            if step < GROUPS:
+                quantise(step)
+            if step >= 2:
+                blend(step - 2)

@@ -126,48 +126,44 @@ def tile_layernormgrucell_pb_t_kernel(
                         scale=-1.0 * WIDTH,
                         accum_out=dev_sq_sum[:, path, t : t + 1],
                     )
-            neg_mean = pairs.tile([P, 2, TILES], F32, name="neg_mean")
-            var_eps = pairs.tile([P, 2, TILES], F32, name="var_eps")
-            rstd = pairs.tile([P, 2, TILES], F32, name="rstd")
-            std_i = pairs.tile([P, TILES], F32, name="std_i")
-            ratio = pairs.tile([P, TILES], F32, name="ratio")
-            shift_i = pairs.tile([P, TILES], F32, name="shift_i")
-            nc.gpsimd.tensor_scalar(
-                out=neg_mean[:], in0=row_sum[:], scalar1=-1.0 / WIDTH, scalar2=0.0,
-                op0=ALU.mult, op1=ALU.add,
+            std = pairs.tile([P, 2, TILES], F32, name="std")
+            neg_mean_h = pairs.tile([P, TILES], F32, name="neg_mean_h")
+            nc.scalar.activation(
+                out=std[:], in_=dev_sq_sum[:], func=ACT.Sqrt, bias=eps_col[:], scale=1.0 / WIDTH**3
             )
-            nc.gpsimd.tensor_scalar(
-                out=var_eps[:], in0=dev_sq_sum[:], scalar1=1.0 / WIDTH**3, scalar2=EPS,
-                op0=ALU.mult, op1=ALU.add,
-            )
-            nc.gpsimd.tensor_tensor(out=rstd[:], in0=var_eps[:], in1=minus_half[:], op=ALU.pow)
-            nc.gpsimd.tensor_mul(out=std_i[:], in0=var_eps[:, 0, :], in1=rstd[:, 0, :])
-            nc.gpsimd.tensor_mul(out=ratio[:], in0=std_i[:], in1=rstd[:, 1, :])
-            nc.gpsimd.tensor_mul(out=shift_i[:], in0=neg_mean[:, 0, :], in1=rstd[:, 0, :])
+            nc.scalar.mul(out=neg_mean_h[:], in_=row_sum[:, 1, :], mul=-1.0 / WIDTH)
             kept["i_pre", g], kept["h_pre", g] = pre
-            kept["neg_mean", g] = neg_mean
-            kept["rstd", g] = rstd
-            kept["ratio", g] = ratio
-            kept["shift_i", g] = shift_i
+            kept["row_sum", g] = row_sum
+            kept["std", g] = std
+            kept["neg_mean_h", g] = neg_mean_h
 
         def candidate(g):
             gated = pairs.tile(group_shape, F32, name="gated")
             mixed = pairs.tile(group_shape, F32, name="mixed")
             cand = pairs.tile(group_shape, F32, name="cand")
+            rstd = pairs.tile([P, 2, TILES], F32, name="rstd")
+            ratio = pairs.tile([P, TILES], F32, name="ratio")
+            shift_i = pairs.tile([P, TILES], F32, name="shift_i")
+            nc.vector.reciprocal(out=rstd[:], in_=kept["std", g][:])
             for t in range(TILES):
                 nc.vector.scalar_tensor_tensor(
                     out=gated[:, t, :],
                     in0=kept["h_pre", g][:, t, :],
-                    scalar=kept["neg_mean", g][:, 1, t : t + 1],
+                    scalar=kept["neg_mean_h", g][:, t : t + 1],
                     in1=kept["r", g][:, t, :],
                     op0=ALU.add,
                     op1=ALU.mult,
                 )
+            nc.vector.tensor_mul(out=ratio[:], in0=kept["std", g][:, 0, :], in1=rstd[:, 1, :])
+            nc.vector.scalar_tensor_tensor(
+                out=shift_i[:], in0=kept["row_sum", g][:, 0, :], scalar=-1.0 / WIDTH,
+                in1=rstd[:, 0, :], op0=ALU.mult, op1=ALU.mult,
+            )
             for t in range(TILES):
                 nc.vector.scalar_tensor_tensor(
                     out=mixed[:, t, :],
                     in0=gated[:, t, :],
-                    scalar=kept["ratio", g][:, t : t + 1],
+                    scalar=ratio[:, t : t + 1],
                     in1=kept["i_pre", g][:, t, :],
                     op0=ALU.mult,
                     op1=ALU.add,
@@ -176,8 +172,8 @@ def tile_layernormgrucell_pb_t_kernel(
                     out=cand[:, t, :],
                     in_=mixed[:, t, :],
                     func=ACT.Tanh,
-                    bias=kept["shift_i", g][:, t : t + 1],
-                    scale=kept["rstd", g][:, 0, t : t + 1],
+                    bias=shift_i[:, t : t + 1],
+                    scale=rstd[:, 0, t : t + 1],
                 )
             kept["cand", g] = cand
 
@@ -197,8 +193,8 @@ def tile_layernormgrucell_pb_t_kernel(
 
         ident = consts.tile([P, P], F32, name="ident")
         make_identity(nc, ident[:])
-        minus_half = consts.tile([P, 2, TILES], F32, name="minus_half")
-        nc.gpsimd.memset(minus_half[:], -0.5)
+        eps_col = consts.tile([P, 1], F32, name="eps_col")
+        nc.vector.memset(eps_col[:], EPS)
 
         w_words = []
         w_scales = []

@@ -177,16 +177,22 @@ def tile_layernormgrucell_pb_t_kernel(
                 )
             kept["cand", g] = cand
 
-        def blend(g):
+        def hold(g):
             held = pairs.tile(group_shape, F32, name="held")
+            for t in range(TILES):
+                nc.gpsimd.tensor_mul(
+                    out=held[:, t, :], in0=kept["z", g][:, t, :], in1=kept["h", g][:, t, :]
+                )
+            kept["held", g] = held
+
+        def blend(g):
             dropped = pairs.tile(group_shape, F32, name="dropped")
             new_state = pairs.tile(group_shape, F32, name="new_state")
-            nc.vector.tensor_mul(out=held[:], in0=kept["z", g][:], in1=kept["h", g][:])
             nc.vector.scalar_tensor_tensor(
                 out=dropped[:], in0=kept["z", g][:], scalar=1.0, in1=kept["cand", g][:],
                 op0=ALU.subtract, op1=ALU.mult,
             )
-            nc.vector.tensor_sub(out=new_state[:], in0=held[:], in1=dropped[:])
+            nc.vector.tensor_sub(out=new_state[:], in0=kept["held", g][:], in1=dropped[:])
             nc.sync.dma_start(out=out_groups[g], in_=new_state[:])
 
         load_activations(0)
@@ -223,6 +229,7 @@ def tile_layernormgrucell_pb_t_kernel(
                 load_activations(step + 1)
             if 1 <= step <= GROUPS:
                 load_gates(step - 1)
+                hold(step - 1)
             if step < GROUPS:
                 turn(step)
             if step >= 2:

@@ -39,28 +39,17 @@ def tile_layernormgrucell_pb_t_kernel(
         ctx.enter_context(tc.manual_schedule())
         consts = ctx.enter_context(tc.tile_pool(name="consts", bufs=1))
         pairs = ctx.enter_context(tc.tile_pool(name="pairs", bufs=2))
-        h_pool = ctx.enter_context(tc.tile_pool(name="h_pool", bufs=4))
+        triples = ctx.enter_context(tc.tile_pool(name="triples", bufs=3))
         scratch = ctx.enter_context(tc.tile_pool(name="scratch", bufs=4))
         psum_turn = ctx.enter_context(tc.psum_pool(name="psum_turn", bufs=3))
         psum_mm = ctx.enter_context(tc.psum_pool(name="psum_mm", bufs=5))
 
         kept = {}
 
-        def load_activations(g):
-            x_sb = pairs.tile(group_shape, BF16, name="x_sb")
-            h_sb = h_pool.tile(group_shape, BF16, name="h_sb")
-            nc.sync.dma_start(out=x_sb[:], in_=x_groups[g])
-            nc.sync.dma_start(out=h_sb[:], in_=h_groups[g])
-            kept["x", g] = x_sb
-            kept["h", g] = h_sb
-
-        def load_gates(g):
-            r_sb = pairs.tile(group_shape, BF16, name="r_sb")
-            z_sb = pairs.tile(group_shape, BF16, name="z_sb")
-            nc.sync.dma_start(out=r_sb[:], in_=r_groups[g])
-            nc.sync.dma_start(out=z_sb[:], in_=z_groups[g])
-            kept["r", g] = r_sb
-            kept["z", g] = z_sb
+        def load(name, pool, groups, g):
+            rows_sb = pool.tile(group_shape, BF16, name=name + "_sb")
+            nc.sync.dma_start(out=rows_sb[:], in_=groups[g])
+            kept[name, g] = rows_sb
 
         def turn(g):
             grouped = pairs.tile([P, TILES, 2, P, PACK], BF16, name="grouped", align_bytes=64)
@@ -88,6 +77,14 @@ def tile_layernormgrucell_pb_t_kernel(
             )
             kept["codes", g] = codes
             kept["code_scales", g] = code_scales
+
+        def hold(g):
+            held = pairs.tile(group_shape, F32, name="held")
+            for t in range(TILES):
+                nc.gpsimd.tensor_mul(
+                    out=held[:, t, :], in0=kept["z", g][:, t, :], in1=kept["h", g][:, t, :]
+                )
+            kept["held", g] = held
 
         def products(g):
             pre = (
@@ -126,14 +123,18 @@ def tile_layernormgrucell_pb_t_kernel(
                         scale=-1.0 * WIDTH,
                         accum_out=dev_sq_sum[:, path, t : t + 1],
                     )
+            kept["i_pre", g], kept["h_pre", g] = pre
+            kept["row_sum", g] = row_sum
+            kept["dev_sq_sum", g] = dev_sq_sum
+
+        def deviations(g):
             std = pairs.tile([P, 2, TILES], F32, name="std")
             neg_mean_h = pairs.tile([P, TILES], F32, name="neg_mean_h")
             nc.scalar.activation(
-                out=std[:], in_=dev_sq_sum[:], func=ACT.Sqrt, bias=eps_col[:], scale=1.0 / WIDTH**3
+                out=std[:], in_=kept["dev_sq_sum", g][:], func=ACT.Sqrt,
+                bias=eps_col[:], scale=1.0 / WIDTH**3,
             )
-            nc.scalar.mul(out=neg_mean_h[:], in_=row_sum[:, 1, :], mul=-1.0 / WIDTH)
-            kept["i_pre", g], kept["h_pre", g] = pre
-            kept["row_sum", g] = row_sum
+            nc.scalar.mul(out=neg_mean_h[:], in_=kept["row_sum", g][:, 1, :], mul=-1.0 / WIDTH)
             kept["std", g] = std
             kept["neg_mean_h", g] = neg_mean_h
 
@@ -177,25 +178,22 @@ def tile_layernormgrucell_pb_t_kernel(
                 )
             kept["cand", g] = cand
 
-        def hold(g):
-            held = pairs.tile(group_shape, F32, name="held")
-            for t in range(TILES):
-                nc.gpsimd.tensor_mul(
-                    out=held[:, t, :], in0=kept["z", g][:, t, :], in1=kept["h", g][:, t, :]
-                )
-            kept["held", g] = held
-
         def blend(g):
             dropped = pairs.tile(group_shape, F32, name="dropped")
             new_state = pairs.tile(group_shape, F32, name="new_state")
-            nc.vector.scalar_tensor_tensor(
-                out=dropped[:], in0=kept["z", g][:], scalar=1.0, in1=kept["cand", g][:],
-                op0=ALU.subtract, op1=ALU.mult,
-            )
-            nc.vector.tensor_sub(out=new_state[:], in0=kept["held", g][:], in1=dropped[:])
-            nc.sync.dma_start(out=out_groups[g], in_=new_state[:])
+            for t in range(TILES):
+                nc.vector.scalar_tensor_tensor(
+                    out=dropped[:, t, :], in0=kept["z", g][:, t, :], scalar=1.0,
+                    in1=kept["cand", g][:, t, :], op0=ALU.subtract, op1=ALU.mult,
+                )
+            for t in range(TILES):
+                nc.vector.tensor_sub(
+                    out=new_state[:, t, :], in0=kept["held", g][:, t, :], in1=dropped[:, t, :]
+                )
+                nc.sync.dma_start(out=out_groups[g][:, t, :], in_=new_state[:, t, :])
 
-        load_activations(0)
+        load("x", pairs, x_groups, 0)
+        load("h", triples, h_groups, 0)
 
         ident = consts.tile([P, P], F32, name="ident")
         make_identity(nc, ident[:])
@@ -226,16 +224,20 @@ def tile_layernormgrucell_pb_t_kernel(
 
         for step in range(GROUPS + 2):
             if step + 1 < GROUPS:
-                load_activations(step + 1)
+                load("x", pairs, x_groups, step + 1)
+                load("h", triples, h_groups, step + 1)
+            if step < GROUPS:
+                load("z", triples, z_groups, step)
             if 1 <= step <= GROUPS:
-                load_gates(step - 1)
+                load("r", pairs, r_groups, step - 1)
                 hold(step - 1)
+                products(step - 1)
             if step < GROUPS:
                 turn(step)
             if step >= 2:
                 candidate(step - 2)
             if 1 <= step <= GROUPS:
-                products(step - 1)
+                deviations(step - 1)
             if step < GROUPS:
                 quantise(step)
             if step >= 2:

@@ -121,31 +121,38 @@ def tile_layernormgrucell_pb_t_kernel(
                         func=ACT.Square,
                         bias=row_sum[:, path, t : t + 1],
                         scale=-1.0 * WIDTH,
-                        accum_out=dev_sq_sum[:, path, t : t + 1],
+                        accum_out=dev_sq_sum[:, 1 - path, t : t + 1],
                     )
             kept["i_pre", g], kept["h_pre", g] = pre
             kept["row_sum", g] = row_sum
             kept["dev_sq_sum", g] = dev_sq_sum
 
         def deviations(g):
-            std = pairs.tile([P, 2, TILES], F32, name="std")
+            log_var = pairs.tile([P, 2, TILES], F32, name="log_var")
+            rstd = pairs.tile([P, 2, TILES], F32, name="rstd")
+            left = pairs.tile([P, 2, TILES], F32, name="left")
             neg_mean_h = pairs.tile([P, TILES], F32, name="neg_mean_h")
             nc.scalar.activation(
-                out=std[:], in_=kept["dev_sq_sum", g][:], func=ACT.Sqrt,
+                out=log_var[:], in_=kept["dev_sq_sum", g][:], func=ACT.Ln,
                 bias=eps_col[:], scale=1.0 / WIDTH**3,
             )
+            nc.scalar.activation(out=rstd[:], in_=log_var[:], func=ACT.Exp, scale=-0.5)
+            nc.scalar.activation(out=left[:, 0, :], in_=log_var[:, 1, :], func=ACT.Exp, scale=0.5)
+            nc.scalar.mul(out=left[:, 1, :], in_=kept["row_sum", g][:, 0, :], mul=-1.0 / WIDTH)
             nc.scalar.mul(out=neg_mean_h[:], in_=kept["row_sum", g][:, 1, :], mul=-1.0 / WIDTH)
-            kept["std", g] = std
+            kept["rstd", g] = rstd
+            kept["left", g] = left
             kept["neg_mean_h", g] = neg_mean_h
 
         def candidate(g):
             gated = pairs.tile(group_shape, F32, name="gated")
             mixed = pairs.tile(group_shape, F32, name="mixed")
             cand = pairs.tile(group_shape, F32, name="cand")
-            rstd = pairs.tile([P, 2, TILES], F32, name="rstd")
-            ratio = pairs.tile([P, TILES], F32, name="ratio")
-            shift_i = pairs.tile([P, TILES], F32, name="shift_i")
-            nc.vector.reciprocal(out=rstd[:], in_=kept["std", g][:])
+            rstd = kept["rstd", g]
+            row_scalars = pairs.tile([P, 2, TILES], F32, name="row_scalars")
+            nc.vector.tensor_mul(out=row_scalars[:], in0=kept["left", g][:], in1=rstd[:])
+            ratio = row_scalars[:, 0, :]
+            shift_i = row_scalars[:, 1, :]
             for t in range(TILES):
                 nc.vector.scalar_tensor_tensor(
                     out=gated[:, t, :],
@@ -155,11 +162,6 @@ def tile_layernormgrucell_pb_t_kernel(
                     op0=ALU.add,
                     op1=ALU.mult,
                 )
-            nc.vector.tensor_mul(out=ratio[:], in0=kept["std", g][:, 0, :], in1=rstd[:, 1, :])
-            nc.vector.scalar_tensor_tensor(
-                out=shift_i[:], in0=kept["row_sum", g][:, 0, :], scalar=-1.0 / WIDTH,
-                in1=rstd[:, 0, :], op0=ALU.mult, op1=ALU.mult,
-            )
             for t in range(TILES):
                 nc.vector.scalar_tensor_tensor(
                     out=mixed[:, t, :],
@@ -174,7 +176,7 @@ def tile_layernormgrucell_pb_t_kernel(
                     in_=mixed[:, t, :],
                     func=ACT.Tanh,
                     bias=shift_i[:, t : t + 1],
-                    scale=rstd[:, 0, t : t + 1],
+                    scale=rstd[:, 1, t : t + 1],
                 )
             kept["cand", g] = cand
 

@@ -80,9 +80,10 @@ def tile_layernormgrucell_pb_t_kernel(
 
         def hold(g):
             held = pairs.tile(group_shape, F32, name="held")
-            for t in range(TILES):
+            for t in range(0, TILES, 2):
                 nc.gpsimd.tensor_mul(
-                    out=held[:, t, :], in0=kept["z", g][:, t, :], in1=kept["h", g][:, t, :]
+                    out=held[:, t : t + 2, :], in0=kept["z", g][:, t : t + 2, :],
+                    in1=kept["h", g][:, t : t + 2, :],
                 )
             kept["held", g] = held
 

from contextlib import ExitStack

import concourse.mybir as mybir
from concourse.masks import make_identity

F32 = mybir.dt.float32
BF16 = mybir.dt.bfloat16
I32 = mybir.dt.int32
U32 = mybir.dt.uint32
U8 = mybir.dt.uint8
FP8X4 = mybir.dt.float8_e4m3fn_x4
FP4X4 = mybir.dt.float4_e2m1fn_x4
ALU = mybir.AluOpType
ACT = mybir.ActivationFunctionType

P = 128
PACK = 4
ROWS = 4096
WIDTH = 512
TILES = 4
GROUPS = ROWS // (P * TILES)
EPS = 1e-5
FLOPS = 2 * 2 * ROWS * WIDTH * WIDTH


def tile_layernormgrucell_pb_t_kernel(
    tc, x, h, r, z, W_in_words, W_in_scales, b_in, W_hn_words, W_hn_scales, b_hn, out
):
    nc = tc.nc
    by_group = "(g p t) n -> g p t n"
    x_groups = x.rearrange(by_group, p=P, t=TILES)
    h_groups = h.rearrange(by_group, p=P, t=TILES)
    r_groups = r.rearrange(by_group, p=P, t=TILES)
    z_groups = z.rearrange(by_group, p=P, t=TILES)
    out_groups = out.rearrange(by_group, p=P, t=TILES)
    group_shape = [P, TILES, WIDTH]

    with ExitStack() as ctx:
        ctx.enter_context(tc.manual_schedule())
        consts = ctx.enter_context(tc.tile_pool(name="consts", bufs=1))
        pairs = ctx.enter_context(tc.tile_pool(name="pairs", bufs=2))
        triples = ctx.enter_context(tc.tile_pool(name="triples", bufs=3))
        scratch = ctx.enter_context(tc.tile_pool(name="scratch", bufs=4))
        psum_turn = ctx.enter_context(tc.psum_pool(name="psum_turn", bufs=3))
        psum_mm = ctx.enter_context(tc.psum_pool(name="psum_mm", bufs=5))

        kept = {}

        def load(name, pool, groups, g):
            rows_sb = pool.tile(group_shape, BF16, name=name + "_sb")
            nc.sync.dma_start(out=rows_sb[:], in_=groups[g])
            kept[name, g] = rows_sb

        def turn(g):
            grouped = pairs.tile([P, TILES, 2, P, PACK], BF16, name="grouped", align_bytes=64)
            for t in range(TILES):
                turned = psum_turn.tile([P, 2, 2, P], F32, name="turned")
                for path, rows_sb in enumerate((kept["x", g], kept["h", g])):
                    row_words = rows_sb[:, t, :].bitcast(F32)
                    for u in range(2):
                        nc.tensor.transpose(
                            turned[:, path, u, :], row_words[:, u : WIDTH // 2 : 2], ident[:]
                        )
                nc.scalar.copy(
                    out=grouped[:, t].bitcast(F32),
                    in_=turned[:].rearrange("p path u row -> p path row u"),
                )
            kept["grouped", g] = grouped

        def quantise(g):
            codes = pairs.tile([P, TILES, 2, P], U32, name="codes", align_bytes=64)
            code_scales = pairs.tile([P, TILES, 2, P], U8, name="code_scales", align_bytes=64)
            nc.vector.quantize_mx(
                out=codes[:].rearrange("p t path row -> p (t path row)").bitcast(FP8X4),
                scales=code_scales[:].rearrange("p t path row -> p (t path row)"),
                in_=kept["grouped", g][:].rearrange("p t path row j -> p (t path row j)"),
            )
            kept["codes", g] = codes
            kept["code_scales", g] = code_scales

        def hold(g):
            held = pairs.tile(group_shape, F32, name="held")
            for t in range(0, TILES, 2):
                nc.gpsimd.tensor_mul(
                    out=held[:, t : t + 2, :], in0=kept["z", g][:, t : t + 2, :],
                    in1=kept["h", g][:, t : t + 2, :],
                )
            kept["held", g] = held

        def products(g):
            pre = (
                pairs.tile(group_shape, F32, name="i_pre"),
                pairs.tile(group_shape, F32, name="h_pre"),
            )
            row_sum = pairs.tile([P, 2, TILES], F32, name="row_sum")
            dev_sq_sum = pairs.tile([P, 2, TILES], F32, name="dev_sq_sum")
            for t in range(TILES):
                for path in range(2):
                    product = psum_mm.tile([P, WIDTH], F32, name="product")
                    nc.tensor.matmul_mx(
                        out=product[:],
                        lhsT=kept["codes", g][:, t, path, :].bitcast(FP8X4),
                        lhsT_scale=kept["code_scales", g][:, t, path, :],
                        rhs=w_words[path][:].bitcast(FP4X4),
                        rhs_scale=w_scales[path][:],
                        start=True,
                        stop=True,
                    )
                    nc.vector.scalar_tensor_tensor(
                        out=pre[path][:, t, :],
                        in0=product[:],
                        scalar=0.0,
                        in1=bias_rows[path][:],
                        op0=ALU.add,
                        op1=ALU.add,
                        accum_out=row_sum[:, path, t : t + 1],
                    )
                    dev_sq = scratch.tile([P, WIDTH], F32, name="dev_sq")
                    nc.scalar.activation(
                        out=dev_sq[:],
                        in_=pre[path][:, t, :],
                        func=ACT.Square,
                        bias=row_sum[:, path, t : t + 1],
                        scale=-1.0 * WIDTH,
                        accum_out=dev_sq_sum[:, 1 - path, t : t + 1],
                    )
            kept["i_pre", g], kept["h_pre", g] = pre
            kept["row_sum", g] = row_sum
            kept["dev_sq_sum", g] = dev_sq_sum

        def deviations(g):
            log_var = pairs.tile([P, 2, TILES], F32, name="log_var")
            rstd = pairs.tile([P, 2, TILES], F32, name="rstd")
            left = pairs.tile([P, 2, TILES], F32, name="left")
            neg_mean_h = pairs.tile([P, TILES], F32, name="neg_mean_h")
            nc.scalar.activation(
                out=log_var[:], in_=kept["dev_sq_sum", g][:], func=ACT.Ln,
                bias=eps_col[:], scale=1.0 / WIDTH**3,
            )
            nc.scalar.activation(out=rstd[:], in_=log_var[:], func=ACT.Exp, scale=-0.5)
            nc.scalar.activation(out=left[:, 0, :], in_=log_var[:, 1, :], func=ACT.Exp, scale=0.5)
            nc.scalar.mul(out=left[:, 1, :], in_=kept["row_sum", g][:, 0, :], mul=-1.0 / WIDTH)
            nc.scalar.mul(out=neg_mean_h[:], in_=kept["row_sum", g][:, 1, :], mul=-1.0 / WIDTH)
            kept["rstd", g] = rstd
            kept["left", g] = left
            kept["neg_mean_h", g] = neg_mean_h

        def candidate(g):
            gated = pairs.tile(group_shape, F32, name="gated")
            mixed = pairs.tile(group_shape, F32, name="mixed")
            cand = pairs.tile(group_shape, F32, name="cand")
            rstd = kept["rstd", g]
            row_scalars = pairs.tile([P, 2, TILES], F32, name="row_scalars")
            nc.vector.tensor_mul(out=row_scalars[:], in0=kept["left", g][:], in1=rstd[:])
            ratio = row_scalars[:, 0, :]
            shift_i = row_scalars[:, 1, :]
            for t in range(TILES):
                nc.vector.scalar_tensor_tensor(
                    out=gated[:, t, :],
                    in0=kept["h_pre", g][:, t, :],
                    scalar=kept["neg_mean_h", g][:, t : t + 1],
                    in1=kept["r", g][:, t, :],
                    op0=ALU.add,
                    op1=ALU.mult,
                )
            for t in range(TILES):
                nc.vector.scalar_tensor_tensor(
                    out=mixed[:, t, :],
                    in0=gated[:, t, :],
                    scalar=ratio[:, t : t + 1],
                    in1=kept["i_pre", g][:, t, :],
                    op0=ALU.mult,
                    op1=ALU.add,
                )
                nc.scalar.activation(
                    out=cand[:, t, :],
                    in_=mixed[:, t, :],
                    func=ACT.Tanh,
                    bias=shift_i[:, t : t + 1],
                    scale=rstd[:, 1, t : t + 1],
                )
            kept["cand", g] = cand

        def blend(g):
            dropped = pairs.tile(group_shape, F32, name="dropped")
            new_state = pairs.tile(group_shape, F32, name="new_state")
            for t in range(TILES):
                nc.vector.scalar_tensor_tensor(
                    out=dropped[:, t, :], in0=kept["z", g][:, t, :], scalar=1.0,
                    in1=kept["cand", g][:, t, :], op0=ALU.subtract, op1=ALU.mult,
                )
            for t in range(TILES):
                nc.vector.tensor_sub(
                    out=new_state[:, t, :], in0=kept["held", g][:, t, :], in1=dropped[:, t, :]
                )
                nc.sync.dma_start(out=out_groups[g][:, t, :], in_=new_state[:, t, :])

        load("x", pairs, x_groups, 0)
        load("h", triples, h_groups, 0)

        ident = consts.tile([P, P], F32, name="ident")
        make_identity(nc, ident[:])
        eps_col = consts.tile([P, 1], F32, name="eps_col")
        nc.vector.memset(eps_col[:], EPS)

        w_words = []
        w_scales = []
        bias_rows = []
        for path, words, scales, bias in (
            ("i", W_in_words, W_in_scales, b_in),
            ("h", W_hn_words, W_hn_scales, b_hn),
        ):
            words_sb = consts.tile([P, 2 * WIDTH], U8, name="w_words_" + path, align_bytes=64)
            nc.sync.dma_start(out=words_sb[:].bitcast(I32), in_=words[0].bitcast(I32))
            scales_sb = consts.tile([P, WIDTH], U8, name="w_scales_" + path, align_bytes=64)
            nc.vector.memset(scales_sb[:].bitcast(I32), 0)
            for quadrant in range(4):
                nc.sync.dma_start(
                    out=scales_sb[32 * quadrant : 32 * quadrant + 4, :].bitcast(I32),
                    in_=scales[0, 4 * quadrant : 4 * quadrant + 4, :].bitcast(I32),
                )
            bias_sb = consts.tile([P, WIDTH], BF16, name="bias_" + path)
            nc.sync.dma_start(out=bias_sb[:], in_=bias.partition_broadcast(P))
            w_words.append(words_sb)
            w_scales.append(scales_sb)
            bias_rows.append(bias_sb)

        for step in range(GROUPS + 2):
            if step + 1 < GROUPS:
                load("x", pairs, x_groups, step + 1)
                load("h", triples, h_groups, step + 1)
            if step < GROUPS:
                load("z", triples, z_groups, step)
            if 1 <= step <= GROUPS:
                load("r", pairs, r_groups, step - 1)
                hold(step - 1)
                products(step - 1)
            if step < GROUPS:
                turn(step)
            if step >= 2:
                candidate(step - 2)
            if 1 <= step <= GROUPS:
                deviations(step - 1)
            if step < GROUPS:
                quantise(step)
            if step >= 2:
                blend(step - 2)
